import numpy as np
import ml_dtypes


def mxq(x, axis, fmt="e4m3"):
    dtype, down = {"e4m3": (ml_dtypes.float8_e4m3fn, 7), "e5m2": (ml_dtypes.float8_e5m2, 14)}[fmt]
    v = np.moveaxis(np.asarray(x, np.float32).astype(ml_dtypes.bfloat16).astype(np.float64), axis, -1)
    blocks = v.reshape(v.shape[:-1] + (-1, 32))
    amax = np.abs(blocks).max(-1, keepdims=True)
    byte = np.maximum(np.where(amax > 0, np.frexp(amax)[1] - 1 + 127, 0) - down, 1)
    scale = np.exp2(byte - 127.0)
    codes = (blocks / scale).astype(np.float32).astype(dtype).astype(np.float64)
    return np.moveaxis((codes * scale).reshape(v.shape), -1, axis)


WIDE = False


def mx_kscale(k):
    if not WIDE:
        return np.ones(k)
    levels = np.array([10, -10, 5, -5, 0])
    if k % 512:
        return np.exp2(np.random.permutation(np.resize(levels, k // 32))).repeat(32)
    a = np.empty((k // 512, 16))
    for p in range(k // 512):
        a[p, :8] = np.random.permutation(np.resize(levels, 8))
        for g in range(8):
            far = levels[np.abs(levels - a[p, g]) >= 10]
            a[p, g + 8] = far[np.random.randint(len(far))]
    return np.exp2(a.ravel()).repeat(32)


BF16 = ml_dtypes.bfloat16


def bf(x):
    return np.asarray(x, np.float32).astype(BF16)


def f64(x):
    return np.asarray(x).astype(np.float64)


B, S, DIM, HID, R, NT = 8, 512, 1024, 512, 128, 3
SCALING = 4.0


def silu(v):
    return v / (1.0 + np.exp(-v))


def lora_out(xa, bw, tw):
    return (xa @ bw) * SCALING * tw[..., None]


def setup_inputs():
    s = mx_kscale(DIM)
    return {"x": bf(np.random.standard_normal((B, S, DIM)) * s),
            "w1": bf(np.random.standard_normal((DIM, HID)) / np.sqrt(DIM) / s[:, None]),
            "w3": bf(np.random.standard_normal((DIM, HID)) / np.sqrt(DIM) / s[:, None]),
            "xa_up": bf(np.random.standard_normal((B, S, R))),
            "b_up": bf(np.random.standard_normal((R, HID)) * 0.2 / np.sqrt(R)),
            "xa_gate": bf(np.random.standard_normal((B, S, R))),
            "b_gate": bf(np.random.standard_normal((R, HID)) * 0.2 / np.sqrt(R)),
            "tw_up": bf(np.random.uniform(size=(B, S))),
            "tw_gate": bf(np.random.uniform(size=(B, S)))}


def reference(x, w1, w3, xa_up, b_up, xa_gate, b_gate, tw_up, tw_gate):
    xq = mxq(f64(x), 2, "e4m3")
    up = (xq @ mxq(f64(w3), 0, "e4m3")) + lora_out(f64(xa_up), f64(b_up), f64(tw_up))
    gate = silu((xq @ mxq(f64(w1), 0, "e4m3")) + lora_out(f64(xa_gate), f64(b_gate), f64(tw_gate)))
    return gate * up

@@ -1,0 +1,249 @@
+from contextlib import ExitStack
+
+import concourse.mybir as mybir
+from concourse.masks import make_identity
+
+F32 = mybir.dt.float32
+BF16 = mybir.dt.bfloat16
+U32 = mybir.dt.uint32
+U8 = mybir.dt.uint8
+FP8X4 = mybir.dt.float8_e4m3fn_x4
+ACT = mybir.ActivationFunctionType
+ALU = mybir.AluOpType
+
+P = 128
+TOKENS = 8 * 512
+DIM = 1024
+HID = 512
+RANK = 128
+PACK = 4
+K_PASS = P * PACK
+PASSES = DIM // K_PASS
+N_TILES = TOKENS // P
+ROUND = 2
+N_ROUNDS = N_TILES // ROUND
+X_LOAD = 4
+XA_LOAD = 8
+FLIPS = 4
+LEAD = 8
+
+FLOPS = 2 * TOKENS * DIM * HID * 2 + 2 * TOKENS * RANK * HID * 2
+
+
+def tile_feedforward_pa_t_kernel(
+    tc, x, w1, w3, xa_up, b_up, xa_gate, b_gate, tw_up, tw_gate, out
+):
+    nc = tc.nc
+
+    x_view = x.flatten_outer_dims().rearrange("(p j) k -> p j k", j=N_TILES)
+    xa_up_view = xa_up.flatten_outer_dims().rearrange("(p j) r -> p j r", j=N_TILES)
+    xa_gate_view = xa_gate.flatten_outer_dims().rearrange("(p j) r -> p j r", j=N_TILES)
+    out_view = out.flatten_outer_dims().rearrange("(p j) h -> p j h", j=N_TILES)
+    tw_up_view = tw_up.rearrange("b (q j) -> (b q) j", j=N_TILES)
+    tw_gate_view = tw_gate.rearrange("b (q j) -> (b q) j", j=N_TILES)
+
+    with ExitStack() as ctx:
+        keep = ctx.enter_context(tc.tile_pool(name="keep", bufs=1))
+        w_stage = ctx.enter_context(tc.tile_pool(name="w_stage", bufs=2))
+        x_stage = ctx.enter_context(tc.tile_pool(name="x_stage", bufs=3))
+        sums = ctx.enter_context(tc.tile_pool(name="sums", bufs=LEAD + 6))
+        psum_ring = ctx.enter_context(tc.psum_pool(name="psum_ring", bufs=6))
+        psum_flip = ctx.enter_context(tc.psum_pool(name="psum_flip", bufs=2))
+        ctx.enter_context(tc.manual_schedule())
+
+        xa_up_sb = keep.tile([P, N_TILES, RANK], BF16)
+        xa_gate_sb = keep.tile([P, N_TILES, RANK], BF16)
+
+        def load_adapter_inputs(first):
+            tiles = slice(first, first + XA_LOAD)
+            nc.sync.dma_start(out=xa_up_sb[:, tiles, :], in_=xa_up_view[:, tiles, :])
+            nc.sync.dma_start(out=xa_gate_sb[:, tiles, :], in_=xa_gate_view[:, tiles, :])
+
+        load_adapter_inputs(0)
+
+        tw_up_bf = keep.tile([P, N_TILES], BF16)
+        tw_gate_bf = keep.tile([P, N_TILES], BF16)
+        b_up_sb = keep.tile([RANK, HID], BF16)
+        b_gate_sb = keep.tile([RANK, HID], BF16)
+        nc.sync.dma_start(out=b_gate_sb[:], in_=b_gate)
+        nc.sync.dma_start(out=b_up_sb[:], in_=b_up)
+        nc.sync.dma_start(out=tw_gate_bf[:], in_=tw_gate_view)
+        nc.sync.dma_start(out=tw_up_bf[:], in_=tw_up_view)
+
+        load_adapter_inputs(XA_LOAD)
+
+        w1_raw = keep.tile([P, PASSES * PACK, HID], BF16)
+        w3_raw = keep.tile([P, PASSES * PACK, HID], BF16)
+        for raw, w in ((w1_raw, w1), (w3_raw, w3)):
+            nc.sync.dma_start(
+                out=raw[:].rearrange("p (g t) c -> p g (t c)", t=PACK),
+                in_=w.rearrange("(g p t) c -> p g (t c)", p=P, t=PACK),
+            )
+
+        x_raw = []
+        for first in range(0, N_TILES, X_LOAD):
+            x_part = keep.tile([P, X_LOAD, DIM], BF16, name="x_part%d" % first)
+            nc.sync.dma_start(out=x_part[:], in_=x_view[:, first : first + X_LOAD, :])
+            x_raw.append(x_part)
+            if first == 0:
+                load_adapter_inputs(2 * XA_LOAD)
+                load_adapter_inputs(3 * XA_LOAD)
+
+        ident_bf = keep.tile([P, P], BF16)
+        ident_f32 = keep.tile([P, P], F32)
+        make_identity(nc, ident_bf[:])
+        make_identity(nc, ident_f32[:])
+
+        zero = keep.tile([P, 1], F32)
+        warm = keep.tile([P, 1], F32)
+        nc.vector.memset(zero[:], 0.0)
+        nc.scalar.activation(out=warm[:], in_=zero[:], func=ACT.Silu)
+
+        tw4_up = keep.tile([P, N_TILES], F32)
+        tw4_gate = keep.tile([P, N_TILES], F32)
+        nc.vector.tensor_scalar(tw4_up[:], tw_up_bf[:], 4.0, None, op0=ALU.mult)
+        nc.vector.tensor_scalar(tw4_gate[:], tw_gate_bf[:], 4.0, None, op0=ALU.mult)
+
+        xaT_up = keep.tile([RANK, N_TILES, P], BF16)
+        xaT_gate = keep.tile([RANK, N_TILES, P], BF16)
+
+        def flip_adapter_inputs(first):
+            for start in range(first, first + XA_LOAD, FLIPS):
+                up_bank = psum_ring.tile([RANK, FLIPS, P], BF16, tag="ring")
+                for i in range(FLIPS):
+                    nc.tensor.transpose(up_bank[:, i, :], xa_up_sb[:, start + i, :], ident_bf[:])
+                nc.vector.tensor_copy(out=xaT_up[:, start : start + FLIPS, :], in_=up_bank[:])
+                gate_bank = psum_ring.tile([RANK, FLIPS, P], BF16, tag="ring")
+                for i in range(FLIPS):
+                    nc.tensor.transpose(gate_bank[:, i, :], xa_gate_sb[:, start + i, :], ident_bf[:])
+                nc.scalar.copy(out=xaT_gate[:, start : start + FLIPS, :], in_=gate_bank[:])
+
+        gate_sum = {}
+        up_sum = {}
+
+        def adapters(j):
+            gate_lora = psum_ring.tile([P, HID], F32, tag="ring")
+            nc.tensor.matmul(gate_lora[:], lhsT=xaT_gate[:, j, :], rhs=b_gate_sb[:], start=True, stop=True)
+            gate_sum[j] = sums.tile([P, HID], F32, name="gate_sum%d" % j, tag="gate_sum")
+            nc.scalar.activation(
+                out=gate_sum[j][:], in_=gate_lora[:], func=ACT.Copy, scale=tw4_gate[:, j : j + 1]
+            )
+            up_lora = psum_ring.tile([P, HID], F32, tag="ring")
+            nc.tensor.matmul(up_lora[:], lhsT=xaT_up[:, j, :], rhs=b_up_sb[:], start=True, stop=True)
+            up_sum[j] = sums.tile([P, HID], F32, name="up_sum%d" % j, tag="up_sum")
+            nc.vector.tensor_scalar(
+                up_sum[j][:], up_lora[:], tw4_up[:, j : j + 1], None, op0=ALU.mult
+            )
+
+        def regroup_weight(raw, copies):
+            grouped = []
+            for g in range(PASSES):
+                rows = raw[:, PACK * g : PACK * (g + 1), :]
+                side_by_side = w_stage.tile([P, HID, PACK], BF16, name="w_grouped%d" % g, align_bytes=64)
+                copies[g](
+                    out=side_by_side[:].rearrange("p (c i) t -> p c t i", i=4),
+                    in_=rows.rearrange("p t (c i) -> p c t i", i=4),
+                )
+                grouped.append(side_by_side)
+            return grouped
+
+        def quantise_weight(grouped, codes, scales):
+            for g in range(PASSES):
+                nc.vector.quantize_mx(
+                    out=codes[:, g, :].bitcast(FP8X4),
+                    scales=scales[:, g, :],
+                    in_=grouped[g][:].rearrange("p c t -> p (c t)"),
+                )
+
+        w1_codes = keep.tile([P, PASSES, HID], U32, align_bytes=64)
+        w1_scales = keep.tile([P, PASSES, HID], U8, align_bytes=64)
+        w3_codes = keep.tile([P, PASSES, HID], U32, align_bytes=64)
+        w3_scales = keep.tile([P, PASSES, HID], U8, align_bytes=64)
+
+        x_grouped = {}
+        x_codes = {}
+        x_scales = {}
+
+        def flip_x(r):
+            x_grouped[r] = x_stage.tile([P, ROUND * DIM], BF16, name="x_grouped%d" % r, tag="x_grouped", align_bytes=64)
+            for a in range(ROUND):
+                part, i = divmod(ROUND * r + a, X_LOAD)
+                words = x_raw[part][:, i, :].bitcast(F32)
+                bank = psum_flip.tile([P, FLIPS, P], F32, tag="flip")
+                for q in range(FLIPS):
+                    g, u = divmod(q, 2)
+                    first = g * 2 * P + u
+                    nc.tensor.transpose(bank[:, q, :], words[:, first : (g + 1) * 2 * P : 2], ident_f32[:])
+                nc.scalar.copy(
+                    out=x_grouped[r][:, a * DIM : (a + 1) * DIM]
+                    .bitcast(F32)
+                    .rearrange("p (g r u) -> p g r u", g=PASSES, u=2),
+                    in_=bank[:].rearrange("p (g u) r -> p g r u", u=2),
+                )
+
+        def quantise_x(r):
+            x_codes[r] = x_stage.tile([P, ROUND, PASSES, P], U32, name="x_codes%d" % r, tag="x_codes", align_bytes=64)
+            x_scales[r] = x_stage.tile([P, ROUND, PASSES, P], U8, name="x_scales%d" % r, tag="x_scales", align_bytes=64)
+            nc.vector.quantize_mx(
+                out=x_codes[r][:].rearrange("p a g r -> p (a g r)").bitcast(FP8X4),
+                scales=x_scales[r][:].rearrange("p a g r -> p (a g r)"),
+                in_=x_grouped[r][:],
+            )
+
+        def project(j, codes, scales):
+            r, a = divmod(j, ROUND)
+            acc = psum_ring.tile([P, HID], F32, tag="ring")
+            for g in range(PASSES):
+                nc.tensor.matmul_mx(
+                    out=acc[:],
+                    lhsT=x_codes[r][:, a, g, :].bitcast(FP8X4),
+                    lhsT_scale=x_scales[r][:, a, g, :],
+                    rhs=codes[:, g, :].bitcast(FP8X4),
+                    rhs_scale=scales[:, g, :],
+                    start=(g == 0),
+                    stop=(g == PASSES - 1),
+                )
+            return acc
+
+        def finish(j):
+            gate_mx = project(j, w1_codes, w1_scales)
+            up_mx = project(j, w3_codes, w3_scales)
+            gate = gate_sum[j][:]
+            h = up_sum[j][:]
+            nc.vector.tensor_tensor(out=gate, in0=gate, in1=gate_mx[:], op=ALU.add)
+            nc.scalar.activation(out=gate, in_=gate, func=ACT.Silu)
+            nc.vector.tensor_tensor(out=h, in0=h, in1=up_mx[:], op=ALU.add)
+            multiplier = nc.vector if j == N_TILES - 1 else nc.gpsimd
+            multiplier.tensor_tensor(out=h, in0=h, in1=gate, op=ALU.mult)
+            nc.sync.dma_start(out=out_view[:, j, :], in_=h)
+
+        flip_adapter_inputs(0)
+        for j in range(0, 2):
+            adapters(j)
+        flip_adapter_inputs(XA_LOAD)
+        for j in range(2, 4):
+            adapters(j)
+        w1_grouped = regroup_weight(w1_raw, (nc.vector.tensor_copy, nc.vector.tensor_copy))
+        for j in range(4, 6):
+            adapters(j)
+        quantise_weight(w1_grouped, w1_codes, w1_scales)
+        w3_grouped = regroup_weight(w3_raw, (nc.vector.tensor_copy, nc.scalar.copy))
+        for j in range(6, LEAD):
+            adapters(j)
+        quantise_weight(w3_grouped, w3_codes, w3_scales)
+        flip_x(0)
+        quantise_x(0)
+        flip_adapter_inputs(2 * XA_LOAD)
+        flip_adapter_inputs(3 * XA_LOAD)
+        for r in range(N_ROUNDS):
+            j = ROUND * r
+            if j + LEAD < N_TILES:
+                adapters(j + LEAD)
+            if r + 1 < N_ROUNDS:
+                flip_x(r + 1)
+            if j + LEAD < N_TILES:
+                adapters(j + LEAD + 1)
+            finish(j)
+            if r + 1 < N_ROUNDS:
+                quantise_x(r + 1)
+            finish(j + 1)

@@ -25,6 +25,7 @@ N_ROUNDS = N_TILES // ROUND
 X_LOAD = 4
 XA_LOAD = 8
 FLIPS = 4
+G_COLS = 128
 LEAD = 8
 
 FLOPS = 2 * TOKENS * DIM * HID * 2 + 2 * TOKENS * RANK * HID * 2
@@ -45,7 +46,7 @@ def tile_feedforward_pa_t_kernel(
     with ExitStack() as ctx:
         keep = ctx.enter_context(tc.tile_pool(name="keep", bufs=1))
         w_stage = ctx.enter_context(tc.tile_pool(name="w_stage", bufs=2))
-        x_stage = ctx.enter_context(tc.tile_pool(name="x_stage", bufs=3))
+        x_stage = ctx.enter_context(tc.tile_pool(name="x_stage", bufs=4))
         sums = ctx.enter_context(tc.tile_pool(name="sums", bufs=LEAD + 6))
         psum_ring = ctx.enter_context(tc.psum_pool(name="psum_ring", bufs=6))
         psum_flip = ctx.enter_context(tc.psum_pool(name="psum_flip", bufs=2))
@@ -107,45 +108,74 @@ def tile_feedforward_pa_t_kernel(
         xaT_up = keep.tile([RANK, N_TILES, P], BF16)
         xaT_gate = keep.tile([RANK, N_TILES, P], BF16)
 
-        def flip_adapter_inputs(first):
-            for start in range(first, first + XA_LOAD, FLIPS):
+        def flip_adapter_inputs(first, up_copy=nc.vector.tensor_copy, gate_copy=nc.scalar.copy, count=XA_LOAD):
+            for start in range(first, first + count, FLIPS):
                 up_bank = psum_ring.tile([RANK, FLIPS, P], BF16, tag="ring")
                 for i in range(FLIPS):
                     nc.tensor.transpose(up_bank[:, i, :], xa_up_sb[:, start + i, :], ident_bf[:])
-                nc.vector.tensor_copy(out=xaT_up[:, start : start + FLIPS, :], in_=up_bank[:])
+                up_copy(out=xaT_up[:, start : start + FLIPS, :], in_=up_bank[:])
                 gate_bank = psum_ring.tile([RANK, FLIPS, P], BF16, tag="ring")
                 for i in range(FLIPS):
                     nc.tensor.transpose(gate_bank[:, i, :], xa_gate_sb[:, start + i, :], ident_bf[:])
-                nc.scalar.copy(out=xaT_gate[:, start : start + FLIPS, :], in_=gate_bank[:])
+                gate_copy(out=xaT_gate[:, start : start + FLIPS, :], in_=gate_bank[:])
 
         gate_sum = {}
         up_sum = {}
 
-        def adapters(j):
-            gate_lora = psum_ring.tile([P, HID], F32, tag="ring")
-            nc.tensor.matmul(gate_lora[:], lhsT=xaT_gate[:, j, :], rhs=b_gate_sb[:], start=True, stop=True)
+        def weigh(on, out, bank, weight):
+            if on == "S":
+                nc.scalar.activation(out=out, in_=bank, func=ACT.Copy, scale=weight)
+            else:
+                nc.vector.tensor_scalar(out, bank, weight, None, op0=ALU.mult)
+
+        def gate_adapter(j, on="S"):
+            bank = psum_ring.tile([P, HID], F32, tag="ring")
+            nc.tensor.matmul(bank[:], lhsT=xaT_gate[:, j, :], rhs=b_gate_sb[:], start=True, stop=True)
             gate_sum[j] = sums.tile([P, HID], F32, name="gate_sum%d" % j, tag="gate_sum")
-            nc.scalar.activation(
-                out=gate_sum[j][:], in_=gate_lora[:], func=ACT.Copy, scale=tw4_gate[:, j : j + 1]
-            )
-            up_lora = psum_ring.tile([P, HID], F32, tag="ring")
-            nc.tensor.matmul(up_lora[:], lhsT=xaT_up[:, j, :], rhs=b_up_sb[:], start=True, stop=True)
+            weigh(on, gate_sum[j][:], bank[:], tw4_gate[:, j : j + 1])
+
+        def up_adapter(j, on="V"):
+            bank = psum_ring.tile([P, HID], F32, tag="ring")
+            nc.tensor.matmul(bank[:], lhsT=xaT_up[:, j, :], rhs=b_up_sb[:], start=True, stop=True)
             up_sum[j] = sums.tile([P, HID], F32, name="up_sum%d" % j, tag="up_sum")
-            nc.vector.tensor_scalar(
-                up_sum[j][:], up_lora[:], tw4_up[:, j : j + 1], None, op0=ALU.mult
-            )
+            weigh(on, up_sum[j][:], bank[:], tw4_up[:, j : j + 1])
+
+        def adapters(j, up_on="V"):
+            gate_adapter(j)
+            up_adapter(j, up_on)
 
         def regroup_weight(raw, copies):
             grouped = []
             for g in range(PASSES):
                 rows = raw[:, PACK * g : PACK * (g + 1), :]
                 side_by_side = w_stage.tile([P, HID, PACK], BF16, name="w_grouped%d" % g, align_bytes=64)
-                copies[g](
-                    out=side_by_side[:].rearrange("p (c i) t -> p c t i", i=4),
-                    in_=rows.rearrange("p t (c i) -> p c t i", i=4),
-                )
+                copies[g](side_by_side, rows)
                 grouped.append(side_by_side)
             return grouped
+
+        def group_on_vector(side_by_side, rows):
+            nc.vector.tensor_copy(
+                out=side_by_side[:].rearrange("p (c i) t -> p c t i", i=4),
+                in_=rows.rearrange("p t (c i) -> p c t i", i=4),
+            )
+
+        def group_on_scalar(side_by_side, rows):
+            nc.scalar.copy(
+                out=side_by_side[:].rearrange("p (c i) t -> p c t i", i=4),
+                in_=rows.rearrange("p t (c i) -> p c t i", i=4),
+            )
+
+        def group_on_gpsimd(side_by_side, rows):
+            for first in range(0, HID, G_COLS):
+                columns = slice(first, first + G_COLS)
+                nc.gpsimd.tensor_scalar(
+                    side_by_side[:, columns, :].rearrange("p (c i) t -> p c t i", i=4),
+                    rows[:, :, columns].rearrange("p t (c i) -> p c t i", i=4),
+                    1.0,
+                    0.0,
+                    op0=ALU.mult,
+                    op1=ALU.add,
+                )
 
         def quantise_weight(grouped, codes, scales):
             for g in range(PASSES):
@@ -164,7 +194,7 @@ def tile_feedforward_pa_t_kernel(
         x_codes = {}
         x_scales = {}
 
-        def flip_x(r):
+        def flip_x(r, copies=(nc.scalar.copy, nc.scalar.copy)):
             x_grouped[r] = x_stage.tile([P, ROUND * DIM], BF16, name="x_grouped%d" % r, tag="x_grouped", align_bytes=64)
             for a in range(ROUND):
                 part, i = divmod(ROUND * r + a, X_LOAD)
@@ -174,7 +204,7 @@ def tile_feedforward_pa_t_kernel(
                     g, u = divmod(q, 2)
                     first = g * 2 * P + u
                     nc.tensor.transpose(bank[:, q, :], words[:, first : (g + 1) * 2 * P : 2], ident_f32[:])
-                nc.scalar.copy(
+                copies[a](
                     out=x_grouped[r][:, a * DIM : (a + 1) * DIM]
                     .bitcast(F32)
                     .rearrange("p (g r u) -> p g r u", g=PASSES, u=2),
@@ -205,17 +235,23 @@ def tile_feedforward_pa_t_kernel(
                 )
             return acc
 
+        def add_gate(j, acc):
+            gate = gate_sum[j][:]
+            nc.vector.tensor_tensor(out=gate, in0=gate, in1=acc[:], op=ALU.add)
+            nc.scalar.activation(out=gate, in_=gate, func=ACT.Silu)
+
+        def add_up(j, acc):
+            h = up_sum[j][:]
+            nc.vector.tensor_tensor(out=h, in0=h, in1=acc[:], op=ALU.add)
+            multiplier = nc.vector if j == N_TILES - 1 else nc.gpsimd
+            multiplier.tensor_tensor(out=h, in0=h, in1=gate_sum[j][:], op=ALU.mult)
+            nc.sync.dma_start(out=out_view[:, j, :], in_=h)
+
         def finish(j):
             gate_mx = project(j, w1_codes, w1_scales)
             up_mx = project(j, w3_codes, w3_scales)
-            gate = gate_sum[j][:]
-            h = up_sum[j][:]
-            nc.vector.tensor_tensor(out=gate, in0=gate, in1=gate_mx[:], op=ALU.add)
-            nc.scalar.activation(out=gate, in_=gate, func=ACT.Silu)
-            nc.vector.tensor_tensor(out=h, in0=h, in1=up_mx[:], op=ALU.add)
-            multiplier = nc.vector if j == N_TILES - 1 else nc.gpsimd
-            multiplier.tensor_tensor(out=h, in0=h, in1=gate, op=ALU.mult)
-            nc.sync.dma_start(out=out_view[:, j, :], in_=h)
+            add_gate(j, gate_mx)
+            add_up(j, up_mx)
 
         flip_adapter_inputs(0)
         for j in range(0, 2):
@@ -223,27 +259,30 @@ def tile_feedforward_pa_t_kernel(
         flip_adapter_inputs(XA_LOAD)
         for j in range(2, 4):
             adapters(j)
-        w1_grouped = regroup_weight(w1_raw, (nc.vector.tensor_copy, nc.vector.tensor_copy))
+        w1_grouped = regroup_weight(w1_raw, (group_on_vector, group_on_gpsimd))
         for j in range(4, 6):
             adapters(j)
-        quantise_weight(w1_grouped, w1_codes, w1_scales)
-        w3_grouped = regroup_weight(w3_raw, (nc.vector.tensor_copy, nc.scalar.copy))
+        w3_grouped = regroup_weight(w3_raw, (group_on_vector, group_on_scalar))
         for j in range(6, LEAD):
             adapters(j)
+        quantise_weight(w1_grouped, w1_codes, w1_scales)
         quantise_weight(w3_grouped, w3_codes, w3_scales)
         flip_x(0)
         quantise_x(0)
-        flip_adapter_inputs(2 * XA_LOAD)
-        flip_adapter_inputs(3 * XA_LOAD)
+        flip_adapter_inputs(2 * XA_LOAD, nc.scalar.copy, nc.scalar.copy)
+        flip_adapter_inputs(3 * XA_LOAD, nc.scalar.copy, nc.scalar.copy)
+        flipped = 1
         for r in range(N_ROUNDS):
             j = ROUND * r
-            if j + LEAD < N_TILES:
+            more = j + LEAD < N_TILES
+            if more:
                 adapters(j + LEAD)
-            if r + 1 < N_ROUNDS:
-                flip_x(r + 1)
-            if j + LEAD < N_TILES:
+            new = [r + 1] if r + 1 < N_ROUNDS else []
+            for n in new:
+                flip_x(n)
+            if more:
                 adapters(j + LEAD + 1)
             finish(j)
-            if r + 1 < N_ROUNDS:
-                quantise_x(r + 1)
+            for n in new:
+                quantise_x(n)
             finish(j + 1)

@@ -259,7 +259,7 @@ def tile_feedforward_pa_t_kernel(
         flip_adapter_inputs(XA_LOAD)
         for j in range(2, 4):
             adapters(j)
-        w1_grouped = regroup_weight(w1_raw, (group_on_vector, group_on_gpsimd))
+        w1_grouped = regroup_weight(w1_raw, (group_on_vector, group_on_vector))
         for j in range(4, 6):
             adapters(j)
         w3_grouped = regroup_weight(w3_raw, (group_on_vector, group_on_scalar))

@@ -25,7 +25,6 @@ N_ROUNDS = N_TILES // ROUND
 X_LOAD = 4
 XA_LOAD = 8
 FLIPS = 4
-G_COLS = 128
 LEAD = 8
 
 FLOPS = 2 * TOKENS * DIM * HID * 2 + 2 * TOKENS * RANK * HID * 2
@@ -45,8 +44,8 @@ def tile_feedforward_pa_t_kernel(
 
     with ExitStack() as ctx:
         keep = ctx.enter_context(tc.tile_pool(name="keep", bufs=1))
-        w_stage = ctx.enter_context(tc.tile_pool(name="w_stage", bufs=2))
-        x_stage = ctx.enter_context(tc.tile_pool(name="x_stage", bufs=4))
+        w_stage = ctx.enter_context(tc.tile_pool(name="w_stage", bufs=4))
+        x_stage = ctx.enter_context(tc.tile_pool(name="x_stage", bufs=3))
         sums = ctx.enter_context(tc.tile_pool(name="sums", bufs=LEAD + 6))
         psum_ring = ctx.enter_context(tc.psum_pool(name="psum_ring", bufs=6))
         psum_flip = ctx.enter_context(tc.psum_pool(name="psum_flip", bufs=2))
@@ -60,35 +59,37 @@ def tile_feedforward_pa_t_kernel(
             nc.sync.dma_start(out=xa_up_sb[:, tiles, :], in_=xa_up_view[:, tiles, :])
             nc.sync.dma_start(out=xa_gate_sb[:, tiles, :], in_=xa_gate_view[:, tiles, :])
 
-        load_adapter_inputs(0)
-
         tw_up_bf = keep.tile([P, N_TILES], BF16)
         tw_gate_bf = keep.tile([P, N_TILES], BF16)
         b_up_sb = keep.tile([RANK, HID], BF16)
         b_gate_sb = keep.tile([RANK, HID], BF16)
+        w1_raw = keep.tile([P, PASSES * PACK, HID], BF16)
+        w3_raw = keep.tile([P, PASSES * PACK, HID], BF16)
+
+        def load_weight_pass(raw, w, g):
+            nc.sync.dma_start(
+                out=raw[:, PACK * g : PACK * (g + 1), :].rearrange("p t c -> p (t c)"),
+                in_=w[K_PASS * g : K_PASS * (g + 1), :].rearrange("(p t) c -> p (t c)", t=PACK),
+            )
+
+        load_adapter_inputs(0)
         nc.sync.dma_start(out=b_gate_sb[:], in_=b_gate)
         nc.sync.dma_start(out=b_up_sb[:], in_=b_up)
         nc.sync.dma_start(out=tw_gate_bf[:], in_=tw_gate_view)
         nc.sync.dma_start(out=tw_up_bf[:], in_=tw_up_view)
-
+        load_weight_pass(w1_raw, w1, 0)
         load_adapter_inputs(XA_LOAD)
-
-        w1_raw = keep.tile([P, PASSES * PACK, HID], BF16)
-        w3_raw = keep.tile([P, PASSES * PACK, HID], BF16)
-        for raw, w in ((w1_raw, w1), (w3_raw, w3)):
-            nc.sync.dma_start(
-                out=raw[:].rearrange("p (g t) c -> p g (t c)", t=PACK),
-                in_=w.rearrange("(g p t) c -> p g (t c)", p=P, t=PACK),
-            )
+        load_weight_pass(w3_raw, w3, 0)
+        load_adapter_inputs(2 * XA_LOAD)
+        load_weight_pass(w1_raw, w1, 1)
+        load_adapter_inputs(3 * XA_LOAD)
+        load_weight_pass(w3_raw, w3, 1)
 
         x_raw = []
         for first in range(0, N_TILES, X_LOAD):
             x_part = keep.tile([P, X_LOAD, DIM], BF16, name="x_part%d" % first)
             nc.sync.dma_start(out=x_part[:], in_=x_view[:, first : first + X_LOAD, :])
             x_raw.append(x_part)
-            if first == 0:
-                load_adapter_inputs(2 * XA_LOAD)
-                load_adapter_inputs(3 * XA_LOAD)
 
         ident_bf = keep.tile([P, P], BF16)
         ident_f32 = keep.tile([P, P], F32)
@@ -108,82 +109,53 @@ def tile_feedforward_pa_t_kernel(
         xaT_up = keep.tile([RANK, N_TILES, P], BF16)
         xaT_gate = keep.tile([RANK, N_TILES, P], BF16)
 
-        def flip_adapter_inputs(first, up_copy=nc.vector.tensor_copy, gate_copy=nc.scalar.copy, count=XA_LOAD):
-            for start in range(first, first + count, FLIPS):
+        def flip_adapter_inputs(first):
+            for start in range(first, first + XA_LOAD, FLIPS):
                 up_bank = psum_ring.tile([RANK, FLIPS, P], BF16, tag="ring")
                 for i in range(FLIPS):
                     nc.tensor.transpose(up_bank[:, i, :], xa_up_sb[:, start + i, :], ident_bf[:])
-                up_copy(out=xaT_up[:, start : start + FLIPS, :], in_=up_bank[:])
+                nc.vector.tensor_copy(out=xaT_up[:, start : start + FLIPS, :], in_=up_bank[:])
                 gate_bank = psum_ring.tile([RANK, FLIPS, P], BF16, tag="ring")
                 for i in range(FLIPS):
                     nc.tensor.transpose(gate_bank[:, i, :], xa_gate_sb[:, start + i, :], ident_bf[:])
-                gate_copy(out=xaT_gate[:, start : start + FLIPS, :], in_=gate_bank[:])
+                nc.scalar.copy(out=xaT_gate[:, start : start + FLIPS, :], in_=gate_bank[:])
 
         gate_sum = {}
         up_sum = {}
 
-        def weigh(on, out, bank, weight):
-            if on == "S":
-                nc.scalar.activation(out=out, in_=bank, func=ACT.Copy, scale=weight)
-            else:
-                nc.vector.tensor_scalar(out, bank, weight, None, op0=ALU.mult)
-
-        def gate_adapter(j, on="S"):
-            bank = psum_ring.tile([P, HID], F32, tag="ring")
-            nc.tensor.matmul(bank[:], lhsT=xaT_gate[:, j, :], rhs=b_gate_sb[:], start=True, stop=True)
+        def adapters(j, up_on_scalar=False):
+            gate_lora = psum_ring.tile([P, HID], F32, tag="ring")
+            nc.tensor.matmul(gate_lora[:], lhsT=xaT_gate[:, j, :], rhs=b_gate_sb[:], start=True, stop=True)
             gate_sum[j] = sums.tile([P, HID], F32, name="gate_sum%d" % j, tag="gate_sum")
-            weigh(on, gate_sum[j][:], bank[:], tw4_gate[:, j : j + 1])
-
-        def up_adapter(j, on="V"):
-            bank = psum_ring.tile([P, HID], F32, tag="ring")
-            nc.tensor.matmul(bank[:], lhsT=xaT_up[:, j, :], rhs=b_up_sb[:], start=True, stop=True)
+            nc.scalar.activation(
+                out=gate_sum[j][:], in_=gate_lora[:], func=ACT.Copy, scale=tw4_gate[:, j : j + 1]
+            )
+            up_lora = psum_ring.tile([P, HID], F32, tag="ring")
+            nc.tensor.matmul(up_lora[:], lhsT=xaT_up[:, j, :], rhs=b_up_sb[:], start=True, stop=True)
             up_sum[j] = sums.tile([P, HID], F32, name="up_sum%d" % j, tag="up_sum")
-            weigh(on, up_sum[j][:], bank[:], tw4_up[:, j : j + 1])
+            if up_on_scalar:
+                nc.scalar.activation(
+                    out=up_sum[j][:], in_=up_lora[:], func=ACT.Copy, scale=tw4_up[:, j : j + 1]
+                )
+            else:
+                nc.vector.tensor_scalar(
+                    up_sum[j][:], up_lora[:], tw4_up[:, j : j + 1], None, op0=ALU.mult
+                )
 
-        def adapters(j, up_on="V"):
-            gate_adapter(j)
-            up_adapter(j, up_on)
-
-        def regroup_weight(raw, copies):
-            grouped = []
-            for g in range(PASSES):
-                rows = raw[:, PACK * g : PACK * (g + 1), :]
-                side_by_side = w_stage.tile([P, HID, PACK], BF16, name="w_grouped%d" % g, align_bytes=64)
-                copies[g](side_by_side, rows)
-                grouped.append(side_by_side)
-            return grouped
-
-        def group_on_vector(side_by_side, rows):
+        def regroup_weight_pass(raw, g):
+            side_by_side = w_stage.tile([P, HID, PACK], BF16, name="side_by_side", align_bytes=64)
             nc.vector.tensor_copy(
                 out=side_by_side[:].rearrange("p (c i) t -> p c t i", i=4),
-                in_=rows.rearrange("p t (c i) -> p c t i", i=4),
+                in_=raw[:, PACK * g : PACK * (g + 1), :].rearrange("p t (c i) -> p c t i", i=4),
             )
+            return side_by_side
 
-        def group_on_scalar(side_by_side, rows):
-            nc.scalar.copy(
-                out=side_by_side[:].rearrange("p (c i) t -> p c t i", i=4),
-                in_=rows.rearrange("p t (c i) -> p c t i", i=4),
+        def quantise_weight_pass(side_by_side, codes, scales, g):
+            nc.vector.quantize_mx(
+                out=codes[:, g, :].bitcast(FP8X4),
+                scales=scales[:, g, :],
+                in_=side_by_side[:].rearrange("p c t -> p (c t)"),
             )
-
-        def group_on_gpsimd(side_by_side, rows):
-            for first in range(0, HID, G_COLS):
-                columns = slice(first, first + G_COLS)
-                nc.gpsimd.tensor_scalar(
-                    side_by_side[:, columns, :].rearrange("p (c i) t -> p c t i", i=4),
-                    rows[:, :, columns].rearrange("p t (c i) -> p c t i", i=4),
-                    1.0,
-                    0.0,
-                    op0=ALU.mult,
-                    op1=ALU.add,
-                )
-
-        def quantise_weight(grouped, codes, scales):
-            for g in range(PASSES):
-                nc.vector.quantize_mx(
-                    out=codes[:, g, :].bitcast(FP8X4),
-                    scales=scales[:, g, :],
-                    in_=grouped[g][:].rearrange("p c t -> p (c t)"),
-                )
 
         w1_codes = keep.tile([P, PASSES, HID], U32, align_bytes=64)
         w1_scales = keep.tile([P, PASSES, HID], U8, align_bytes=64)
@@ -194,7 +166,7 @@ def tile_feedforward_pa_t_kernel(
         x_codes = {}
         x_scales = {}
 
-        def flip_x(r, copies=(nc.scalar.copy, nc.scalar.copy)):
+        def flip_x(r):
             x_grouped[r] = x_stage.tile([P, ROUND * DIM], BF16, name="x_grouped%d" % r, tag="x_grouped", align_bytes=64)
             for a in range(ROUND):
                 part, i = divmod(ROUND * r + a, X_LOAD)
@@ -204,7 +176,7 @@ def tile_feedforward_pa_t_kernel(
                     g, u = divmod(q, 2)
                     first = g * 2 * P + u
                     nc.tensor.transpose(bank[:, q, :], words[:, first : (g + 1) * 2 * P : 2], ident_f32[:])
-                copies[a](
+                nc.scalar.copy(
                     out=x_grouped[r][:, a * DIM : (a + 1) * DIM]
                     .bitcast(F32)
                     .rearrange("p (g r u) -> p g r u", g=PASSES, u=2),
@@ -235,54 +207,44 @@ def tile_feedforward_pa_t_kernel(
                 )
             return acc
 
-        def add_gate(j, acc):
-            gate = gate_sum[j][:]
-            nc.vector.tensor_tensor(out=gate, in0=gate, in1=acc[:], op=ALU.add)
-            nc.scalar.activation(out=gate, in_=gate, func=ACT.Silu)
-
-        def add_up(j, acc):
-            h = up_sum[j][:]
-            nc.vector.tensor_tensor(out=h, in0=h, in1=acc[:], op=ALU.add)
-            multiplier = nc.vector if j == N_TILES - 1 else nc.gpsimd
-            multiplier.tensor_tensor(out=h, in0=h, in1=gate_sum[j][:], op=ALU.mult)
-            nc.sync.dma_start(out=out_view[:, j, :], in_=h)
-
         def finish(j):
             gate_mx = project(j, w1_codes, w1_scales)
             up_mx = project(j, w3_codes, w3_scales)
-            add_gate(j, gate_mx)
-            add_up(j, up_mx)
+            gate = gate_sum[j][:]
+            h = up_sum[j][:]
+            nc.vector.tensor_tensor(out=gate, in0=gate, in1=gate_mx[:], op=ALU.add)
+            nc.scalar.activation(out=gate, in_=gate, func=ACT.Silu)
+            nc.vector.tensor_tensor(out=h, in0=h, in1=up_mx[:], op=ALU.add)
+            multiplier = nc.vector if j == N_TILES - 1 else nc.gpsimd
+            multiplier.tensor_tensor(out=h, in0=h, in1=gate, op=ALU.mult)
+            nc.sync.dma_start(out=out_view[:, j, :], in_=h)
 
-        flip_adapter_inputs(0)
-        for j in range(0, 2):
-            adapters(j)
-        flip_adapter_inputs(XA_LOAD)
-        for j in range(2, 4):
-            adapters(j)
-        w1_grouped = regroup_weight(w1_raw, (group_on_vector, group_on_vector))
-        for j in range(4, 6):
-            adapters(j)
-        w3_grouped = regroup_weight(w3_raw, (group_on_vector, group_on_scalar))
-        for j in range(6, LEAD):
-            adapters(j)
-        quantise_weight(w1_grouped, w1_codes, w1_scales)
-        quantise_weight(w3_grouped, w3_codes, w3_scales)
-        flip_x(0)
-        quantise_x(0)
-        flip_adapter_inputs(2 * XA_LOAD, nc.scalar.copy, nc.scalar.copy)
-        flip_adapter_inputs(3 * XA_LOAD, nc.scalar.copy, nc.scalar.copy)
-        flipped = 1
+        weight_passes = [
+            (raw, codes, scales, g)
+            for g in range(PASSES)
+            for raw, codes, scales in (
+                (w1_raw, w1_codes, w1_scales),
+                (w3_raw, w3_codes, w3_scales),
+            )
+        ]
+        for step, (raw, codes, scales, g) in enumerate(weight_passes):
+            flip_adapter_inputs(step * XA_LOAD)
+            side_by_side = regroup_weight_pass(raw, g)
+            adapters(2 * step)
+            if step == len(weight_passes) - 1:
+                flip_x(0)
+                quantise_x(0)
+            quantise_weight_pass(side_by_side, codes, scales, g)
+            adapters(2 * step + 1, up_on_scalar=True)
         for r in range(N_ROUNDS):
             j = ROUND * r
-            more = j + LEAD < N_TILES
-            if more:
+            if j + LEAD < N_TILES:
                 adapters(j + LEAD)
-            new = [r + 1] if r + 1 < N_ROUNDS else []
-            for n in new:
-                flip_x(n)
-            if more:
+            if r + 1 < N_ROUNDS:
+                flip_x(r + 1)
+            if j + LEAD < N_TILES:
                 adapters(j + LEAD + 1)
             finish(j)
-            for n in new:
-                quantise_x(n)
+            if r + 1 < N_ROUNDS:
+                quantise_x(r + 1)
             finish(j + 1)

@@ -22,7 +22,7 @@ PASSES = DIM // K_PASS
 N_TILES = TOKENS // P
 ROUND = 2
 N_ROUNDS = N_TILES // ROUND
-X_LOAD = 4
+X_LOAD = 2
 XA_LOAD = 8
 FLIPS = 4
 LEAD = 8
@@ -46,7 +46,7 @@ def tile_feedforward_pa_t_kernel(
         keep = ctx.enter_context(tc.tile_pool(name="keep", bufs=1))
         w_stage = ctx.enter_context(tc.tile_pool(name="w_stage", bufs=4))
         x_stage = ctx.enter_context(tc.tile_pool(name="x_stage", bufs=3))
-        sums = ctx.enter_context(tc.tile_pool(name="sums", bufs=LEAD + 6))
+        sums = ctx.enter_context(tc.tile_pool(name="sums", bufs=LEAD + 10))
         psum_ring = ctx.enter_context(tc.psum_pool(name="psum_ring", bufs=6))
         psum_flip = ctx.enter_context(tc.psum_pool(name="psum_flip", bufs=2))
         ctx.enter_context(tc.manual_schedule())
@@ -86,10 +86,15 @@ def tile_feedforward_pa_t_kernel(
         load_weight_pass(w3_raw, w3, 1)
 
         x_raw = []
-        for first in range(0, N_TILES, X_LOAD):
+
+        def load_x():
+            first = X_LOAD * len(x_raw)
             x_part = keep.tile([P, X_LOAD, DIM], BF16, name="x_part%d" % first)
             nc.sync.dma_start(out=x_part[:], in_=x_view[:, first : first + X_LOAD, :])
             x_raw.append(x_part)
+
+        for part in range(6):
+            load_x()
 
         ident_bf = keep.tile([P, P], BF16)
         ident_f32 = keep.tile([P, P], F32)
@@ -192,32 +197,59 @@ def tile_feedforward_pa_t_kernel(
                 in_=x_grouped[r][:],
             )
 
-        def project(j, codes, scales):
+        def project(j, codes, scales, first=0, width=HID):
             r, a = divmod(j, ROUND)
-            acc = psum_ring.tile([P, HID], F32, tag="ring")
+            columns = slice(first, first + width)
+            acc = psum_ring.tile([P, width], F32, tag="ring")
             for g in range(PASSES):
                 nc.tensor.matmul_mx(
                     out=acc[:],
                     lhsT=x_codes[r][:, a, g, :].bitcast(FP8X4),
                     lhsT_scale=x_scales[r][:, a, g, :],
-                    rhs=codes[:, g, :].bitcast(FP8X4),
-                    rhs_scale=scales[:, g, :],
+                    rhs=codes[:, g, columns].bitcast(FP8X4),
+                    rhs_scale=scales[:, g, columns],
                     start=(g == 0),
                     stop=(g == PASSES - 1),
                 )
             return acc
 
+        def add_gate(j, gate_mx):
+            gate = gate_sum[j][:]
+            nc.vector.tensor_tensor(out=gate, in0=gate, in1=gate_mx[:], op=ALU.add)
+            nc.scalar.activation(out=gate, in_=gate, func=ACT.Silu)
+
+        def add_up(j, up_mx, first=0, width=HID):
+            h = up_sum[j][:, first : first + width]
+            nc.vector.tensor_tensor(out=h, in0=h, in1=up_mx[:], op=ALU.add)
+
+        def multiply_and_store(j, multiplier, first=0, width=HID):
+            columns = slice(first, first + width)
+            h = up_sum[j][:, columns]
+            multiplier.tensor_tensor(out=h, in0=h, in1=gate_sum[j][:, columns], op=ALU.mult)
+            nc.sync.dma_start(out=out_view[:, j, columns], in_=h)
+
         def finish(j):
             gate_mx = project(j, w1_codes, w1_scales)
             up_mx = project(j, w3_codes, w3_scales)
-            gate = gate_sum[j][:]
-            h = up_sum[j][:]
-            nc.vector.tensor_tensor(out=gate, in0=gate, in1=gate_mx[:], op=ALU.add)
-            nc.scalar.activation(out=gate, in_=gate, func=ACT.Silu)
-            nc.vector.tensor_tensor(out=h, in0=h, in1=up_mx[:], op=ALU.add)
-            multiplier = nc.vector if j == N_TILES - 1 else nc.gpsimd
-            multiplier.tensor_tensor(out=h, in0=h, in1=gate, op=ALU.mult)
-            nc.sync.dma_start(out=out_view[:, j, :], in_=h)
+            add_gate(j, gate_mx)
+            add_up(j, up_mx)
+            multiply_and_store(j, nc.gpsimd)
+
+        def finish_last_round():
+            j, last = N_TILES - 2, N_TILES - 1
+            halves = [(k * HID // 2, HID // 2) for k in range(2)]
+            gate_mx = project(j, w1_codes, w1_scales)
+            up_mx = project(j, w3_codes, w3_scales)
+            last_gate_mx = project(last, w1_codes, w1_scales)
+            last_up_mx = [project(last, w3_codes, w3_scales, *half) for half in halves]
+            add_gate(j, gate_mx)
+            add_up(j, up_mx)
+            add_gate(last, last_gate_mx)
+            multiply_and_store(j, nc.vector)
+            for half, acc in zip(halves, last_up_mx):
+                add_up(last, acc, *half)
+            for half in halves:
+                multiply_and_store(last, nc.vector, *half)
 
         weight_passes = [
             (raw, codes, scales, g)
@@ -238,13 +270,16 @@ def tile_feedforward_pa_t_kernel(
             adapters(2 * step + 1, up_on_scalar=True)
         for r in range(N_ROUNDS):
             j = ROUND * r
+            if j % X_LOAD == 0 and X_LOAD * len(x_raw) < N_TILES:
+                load_x()
             if j + LEAD < N_TILES:
                 adapters(j + LEAD)
             if r + 1 < N_ROUNDS:
                 flip_x(r + 1)
             if j + LEAD < N_TILES:
-                adapters(j + LEAD + 1)
-            finish(j)
+                adapters(j + LEAD + 1, up_on_scalar=r % 2 == 0)
             if r + 1 < N_ROUNDS:
+                finish(j)
                 quantise_x(r + 1)
-            finish(j + 1)
+                finish(j + 1)
+        finish_last_round()

from contextlib import ExitStack

import concourse.mybir as mybir
from concourse.masks import make_identity

F32 = mybir.dt.float32
BF16 = mybir.dt.bfloat16
U32 = mybir.dt.uint32
U8 = mybir.dt.uint8
FP8X4 = mybir.dt.float8_e4m3fn_x4
ACT = mybir.ActivationFunctionType
ALU = mybir.AluOpType

P = 128
TOKENS = 8 * 512
DIM = 1024
HID = 512
RANK = 128
PACK = 4
K_PASS = P * PACK
PASSES = DIM // K_PASS
N_TILES = TOKENS // P
ROUND = 2
N_ROUNDS = N_TILES // ROUND
X_LOAD = 2
XA_LOAD = 8
FLIPS = 4
LEAD = 8

FLOPS = 2 * TOKENS * DIM * HID * 2 + 2 * TOKENS * RANK * HID * 2


def tile_feedforward_pa_t_kernel(
    tc, x, w1, w3, xa_up, b_up, xa_gate, b_gate, tw_up, tw_gate, out
):
    nc = tc.nc

    x_view = x.flatten_outer_dims().rearrange("(p j) k -> p j k", j=N_TILES)
    xa_up_view = xa_up.flatten_outer_dims().rearrange("(p j) r -> p j r", j=N_TILES)
    xa_gate_view = xa_gate.flatten_outer_dims().rearrange("(p j) r -> p j r", j=N_TILES)
    out_view = out.flatten_outer_dims().rearrange("(p j) h -> p j h", j=N_TILES)
    tw_up_view = tw_up.rearrange("b (q j) -> (b q) j", j=N_TILES)
    tw_gate_view = tw_gate.rearrange("b (q j) -> (b q) j", j=N_TILES)

    with ExitStack() as ctx:
        keep = ctx.enter_context(tc.tile_pool(name="keep", bufs=1))
        w_stage = ctx.enter_context(tc.tile_pool(name="w_stage", bufs=4))
        x_stage = ctx.enter_context(tc.tile_pool(name="x_stage", bufs=3))
        sums = ctx.enter_context(tc.tile_pool(name="sums", bufs=LEAD + 10))
        psum_ring = ctx.enter_context(tc.psum_pool(name="psum_ring", bufs=6))
        psum_flip = ctx.enter_context(tc.psum_pool(name="psum_flip", bufs=2))
        ctx.enter_context(tc.manual_schedule())

        xa_up_sb = keep.tile([P, N_TILES, RANK], BF16)
        xa_gate_sb = keep.tile([P, N_TILES, RANK], BF16)

        def load_adapter_inputs(first):
            tiles = slice(first, first + XA_LOAD)
            nc.sync.dma_start(out=xa_up_sb[:, tiles, :], in_=xa_up_view[:, tiles, :])
            nc.sync.dma_start(out=xa_gate_sb[:, tiles, :], in_=xa_gate_view[:, tiles, :])

        tw_up_bf = keep.tile([P, N_TILES], BF16)
        tw_gate_bf = keep.tile([P, N_TILES], BF16)
        b_up_sb = keep.tile([RANK, HID], BF16)
        b_gate_sb = keep.tile([RANK, HID], BF16)
        w1_raw = keep.tile([P, PASSES * PACK, HID], BF16)
        w3_raw = keep.tile([P, PASSES * PACK, HID], BF16)

        def load_weight_pass(raw, w, g):
            nc.sync.dma_start(
                out=raw[:, PACK * g : PACK * (g + 1), :].rearrange("p t c -> p (t c)"),
                in_=w[K_PASS * g : K_PASS * (g + 1), :].rearrange("(p t) c -> p (t c)", t=PACK),
            )

        load_adapter_inputs(0)
        nc.sync.dma_start(out=b_gate_sb[:], in_=b_gate)
        nc.sync.dma_start(out=b_up_sb[:], in_=b_up)
        nc.sync.dma_start(out=tw_gate_bf[:], in_=tw_gate_view)
        nc.sync.dma_start(out=tw_up_bf[:], in_=tw_up_view)
        load_weight_pass(w1_raw, w1, 0)
        load_adapter_inputs(XA_LOAD)
        load_weight_pass(w3_raw, w3, 0)
        load_adapter_inputs(2 * XA_LOAD)
        load_weight_pass(w1_raw, w1, 1)
        load_adapter_inputs(3 * XA_LOAD)
        load_weight_pass(w3_raw, w3, 1)

        x_raw = []

        def load_x():
            first = X_LOAD * len(x_raw)
            x_part = keep.tile([P, X_LOAD, DIM], BF16, name="x_part%d" % first)
            nc.sync.dma_start(out=x_part[:], in_=x_view[:, first : first + X_LOAD, :])
            x_raw.append(x_part)

        for part in range(6):
            load_x()

        ident_bf = keep.tile([P, P], BF16)
        ident_f32 = keep.tile([P, P], F32)
        make_identity(nc, ident_bf[:])
        make_identity(nc, ident_f32[:])

        zero = keep.tile([P, 1], F32)
        warm = keep.tile([P, 1], F32)
        nc.vector.memset(zero[:], 0.0)
        nc.scalar.activation(out=warm[:], in_=zero[:], func=ACT.Silu)

        tw4_up = keep.tile([P, N_TILES], F32)
        tw4_gate = keep.tile([P, N_TILES], F32)
        nc.vector.tensor_scalar(tw4_up[:], tw_up_bf[:], 4.0, None, op0=ALU.mult)
        nc.vector.tensor_scalar(tw4_gate[:], tw_gate_bf[:], 4.0, None, op0=ALU.mult)

        xaT_up = keep.tile([RANK, N_TILES, P], BF16)
        xaT_gate = keep.tile([RANK, N_TILES, P], BF16)

        def flip_adapter_inputs(first):
            for start in range(first, first + XA_LOAD, FLIPS):
                up_bank = psum_ring.tile([RANK, FLIPS, P], BF16, tag="ring")
                for i in range(FLIPS):
                    nc.tensor.transpose(up_bank[:, i, :], xa_up_sb[:, start + i, :], ident_bf[:])
                nc.vector.tensor_copy(out=xaT_up[:, start : start + FLIPS, :], in_=up_bank[:])
                gate_bank = psum_ring.tile([RANK, FLIPS, P], BF16, tag="ring")
                for i in range(FLIPS):
                    nc.tensor.transpose(gate_bank[:, i, :], xa_gate_sb[:, start + i, :], ident_bf[:])
                nc.scalar.copy(out=xaT_gate[:, start : start + FLIPS, :], in_=gate_bank[:])

        gate_sum = {}
        up_sum = {}

        def adapters(j, up_on_scalar=False):
            gate_lora = psum_ring.tile([P, HID], F32, tag="ring")
            nc.tensor.matmul(gate_lora[:], lhsT=xaT_gate[:, j, :], rhs=b_gate_sb[:], start=True, stop=True)
            gate_sum[j] = sums.tile([P, HID], F32, name="gate_sum%d" % j, tag="gate_sum")
            nc.scalar.activation(
                out=gate_sum[j][:], in_=gate_lora[:], func=ACT.Copy, scale=tw4_gate[:, j : j + 1]
            )
            up_lora = psum_ring.tile([P, HID], F32, tag="ring")
            nc.tensor.matmul(up_lora[:], lhsT=xaT_up[:, j, :], rhs=b_up_sb[:], start=True, stop=True)
            up_sum[j] = sums.tile([P, HID], F32, name="up_sum%d" % j, tag="up_sum")
            if up_on_scalar:
                nc.scalar.activation(
                    out=up_sum[j][:], in_=up_lora[:], func=ACT.Copy, scale=tw4_up[:, j : j + 1]
                )
            else:
                nc.vector.tensor_scalar(
                    up_sum[j][:], up_lora[:], tw4_up[:, j : j + 1], None, op0=ALU.mult
                )

        def regroup_weight_pass(raw, g):
            side_by_side = w_stage.tile([P, HID, PACK], BF16, name="side_by_side", align_bytes=64)
            nc.vector.tensor_copy(
                out=side_by_side[:].rearrange("p (c i) t -> p c t i", i=4),
                in_=raw[:, PACK * g : PACK * (g + 1), :].rearrange("p t (c i) -> p c t i", i=4),
            )
            return side_by_side

        def quantise_weight_pass(side_by_side, codes, scales, g):
            nc.vector.quantize_mx(
                out=codes[:, g, :].bitcast(FP8X4),
                scales=scales[:, g, :],
                in_=side_by_side[:].rearrange("p c t -> p (c t)"),
            )

        w1_codes = keep.tile([P, PASSES, HID], U32, align_bytes=64)
        w1_scales = keep.tile([P, PASSES, HID], U8, align_bytes=64)
        w3_codes = keep.tile([P, PASSES, HID], U32, align_bytes=64)
        w3_scales = keep.tile([P, PASSES, HID], U8, align_bytes=64)

        x_grouped = {}
        x_codes = {}
        x_scales = {}

        def flip_x(r):
            x_grouped[r] = x_stage.tile([P, ROUND * DIM], BF16, name="x_grouped%d" % r, tag="x_grouped", align_bytes=64)
            for a in range(ROUND):
                part, i = divmod(ROUND * r + a, X_LOAD)
                words = x_raw[part][:, i, :].bitcast(F32)
                bank = psum_flip.tile([P, FLIPS, P], F32, tag="flip")
                for q in range(FLIPS):
                    g, u = divmod(q, 2)
                    first = g * 2 * P + u
                    nc.tensor.transpose(bank[:, q, :], words[:, first : (g + 1) * 2 * P : 2], ident_f32[:])
                nc.scalar.copy(
                    out=x_grouped[r][:, a * DIM : (a + 1) * DIM]
                    .bitcast(F32)
                    .rearrange("p (g r u) -> p g r u", g=PASSES, u=2),
                    in_=bank[:].rearrange("p (g u) r -> p g r u", u=2),
                )

        def quantise_x(r):
            x_codes[r] = x_stage.tile([P, ROUND, PASSES, P], U32, name="x_codes%d" % r, tag="x_codes", align_bytes=64)
            x_scales[r] = x_stage.tile([P, ROUND, PASSES, P], U8, name="x_scales%d" % r, tag="x_scales", align_bytes=64)
            nc.vector.quantize_mx(
                out=x_codes[r][:].rearrange("p a g r -> p (a g r)").bitcast(FP8X4),
                scales=x_scales[r][:].rearrange("p a g r -> p (a g r)"),
                in_=x_grouped[r][:],
            )

        def project(j, codes, scales, first=0, width=HID):
            r, a = divmod(j, ROUND)
            columns = slice(first, first + width)
            acc = psum_ring.tile([P, width], F32, tag="ring")
            for g in range(PASSES):
                nc.tensor.matmul_mx(
                    out=acc[:],
                    lhsT=x_codes[r][:, a, g, :].bitcast(FP8X4),
                    lhsT_scale=x_scales[r][:, a, g, :],
                    rhs=codes[:, g, columns].bitcast(FP8X4),
                    rhs_scale=scales[:, g, columns],
                    start=(g == 0),
                    stop=(g == PASSES - 1),
                )
            return acc

        def add_gate(j, gate_mx):
            gate = gate_sum[j][:]
            nc.vector.tensor_tensor(out=gate, in0=gate, in1=gate_mx[:], op=ALU.add)
            nc.scalar.activation(out=gate, in_=gate, func=ACT.Silu)

        def add_up(j, up_mx, first=0, width=HID):
            h = up_sum[j][:, first : first + width]
            nc.vector.tensor_tensor(out=h, in0=h, in1=up_mx[:], op=ALU.add)

        def multiply_and_store(j, multiplier, first=0, width=HID):
            columns = slice(first, first + width)
            h = up_sum[j][:, columns]
            multiplier.tensor_tensor(out=h, in0=h, in1=gate_sum[j][:, columns], op=ALU.mult)
            nc.sync.dma_start(out=out_view[:, j, columns], in_=h)

        def finish(j):
            gate_mx = project(j, w1_codes, w1_scales)
            up_mx = project(j, w3_codes, w3_scales)
            add_gate(j, gate_mx)
            add_up(j, up_mx)
            multiply_and_store(j, nc.gpsimd)

        def finish_last_round():
            j, last = N_TILES - 2, N_TILES - 1
            halves = [(k * HID // 2, HID // 2) for k in range(2)]
            gate_mx = project(j, w1_codes, w1_scales)
            up_mx = project(j, w3_codes, w3_scales)
            last_gate_mx = project(last, w1_codes, w1_scales)
            last_up_mx = [project(last, w3_codes, w3_scales, *half) for half in halves]
            add_gate(j, gate_mx)
            add_up(j, up_mx)
            add_gate(last, last_gate_mx)
            multiply_and_store(j, nc.vector)
            for half, acc in zip(halves, last_up_mx):
                add_up(last, acc, *half)
            for half in halves:
                multiply_and_store(last, nc.vector, *half)

        weight_passes = [
            (raw, codes, scales, g)
            for g in range(PASSES)
            for raw, codes, scales in (
                (w1_raw, w1_codes, w1_scales),
                (w3_raw, w3_codes, w3_scales),
            )
        ]
        for step, (raw, codes, scales, g) in enumerate(weight_passes):
            flip_adapter_inputs(step * XA_LOAD)
            side_by_side = regroup_weight_pass(raw, g)
            adapters(2 * step)
            if step == len(weight_passes) - 1:
                flip_x(0)
                quantise_x(0)
            quantise_weight_pass(side_by_side, codes, scales, g)
            adapters(2 * step + 1, up_on_scalar=True)
        for r in range(N_ROUNDS):
            j = ROUND * r
            if j % X_LOAD == 0 and X_LOAD * len(x_raw) < N_TILES:
                load_x()
            if j + LEAD < N_TILES:
                adapters(j + LEAD)
            if r + 1 < N_ROUNDS:
                flip_x(r + 1)
            if j + LEAD < N_TILES:
                adapters(j + LEAD + 1, up_on_scalar=r % 2 == 0)
            if r + 1 < N_ROUNDS:
                finish(j)
                quantise_x(r + 1)
                finish(j + 1)
        finish_last_round()
